import numpy as np
import ml_dtypes


def mxq(x, axis, fmt="e4m3"):
    dtype, down = {"e4m3": (ml_dtypes.float8_e4m3fn, 7), "e5m2": (ml_dtypes.float8_e5m2, 14)}[fmt]
    v = np.moveaxis(np.asarray(x, np.float32).astype(ml_dtypes.bfloat16).astype(np.float64), axis, -1)
    blocks = v.reshape(v.shape[:-1] + (-1, 32))
    amax = np.abs(blocks).max(-1, keepdims=True)
    byte = np.maximum(np.where(amax > 0, np.frexp(amax)[1] - 1 + 127, 0) - down, 1)
    scale = np.exp2(byte - 127.0)
    codes = (blocks / scale).astype(np.float32).astype(dtype).astype(np.float64)
    return np.moveaxis((codes * scale).reshape(v.shape), -1, axis)


WIDE = False


def mx_kscale(k):
    if not WIDE:
        return np.ones(k)
    levels = np.array([10, -10, 5, -5, 0])
    a = np.random.permutation(np.resize(levels, k // 512 * 4)).reshape(k // 512, 4)
    idx = np.arange(k)
    return np.exp2(a[idx // 512, idx % 128 // 32])


BF16 = ml_dtypes.bfloat16


def bf(x):
    return np.asarray(x, np.float32).astype(BF16)


def f64(x):
    return np.asarray(x).astype(np.float64)


E2M1 = np.array([0.0, 0.5, 1.0, 1.5, 2.0, 3.0, 4.0, 6.0, -0.0, -0.5, -1.0, -1.5, -2.0, -3.0, -4.0, -6.0])


def pack_weight(w, fmt):
    k, n = w.shape
    w = f64(bf(w)).reshape(k // 32, 32, n)
    amax = np.abs(w).max(1)
    if fmt == "e4m3":
        byte = np.frexp(amax)[1] - 1 + 127 - 7
    else:
        mant, ex = np.frexp(amax / 6.0)
        byte = np.where(mant > 0.5, ex, ex - 1) + 127
    byte = np.clip(np.where(amax > 0, byte, 1), 1, 254)
    scaled = (w * np.exp2(127.0 - byte)[:, None, :]).reshape(k, n).astype(np.float32)
    by_word = np.ascontiguousarray(scaled.reshape(k // 512, 128, 4, n).transpose(0, 1, 3, 2))
    if fmt == "e4m3":
        words = by_word.astype(ml_dtypes.float8_e4m3fn).view(np.uint8)
    else:
        c = by_word.astype(ml_dtypes.float4_e2m1fn).view(np.uint8) & 0xF
        words = c[..., 0::2] | (c[..., 1::2] << 4)
    return np.ascontiguousarray(words), np.ascontiguousarray(byte.astype(np.uint8).reshape(k // 512, 16, n))


def unpack_weight(words, scales, fmt):
    g, p, n, _ = words.shape
    if fmt == "e4m3":
        vals = np.ascontiguousarray(words).view(ml_dtypes.float8_e4m3fn).astype(np.float64)
    else:
        nib = np.empty((g, p, n, 4), np.uint8)
        nib[..., 0::2] = words & 0xF
        nib[..., 1::2] = words >> 4
        vals = E2M1[nib]
    vals = vals * np.repeat(np.exp2(scales.astype(np.float64) - 127.0), 8, axis=1)[..., None]
    return vals.transpose(0, 1, 3, 2).reshape(g * 512, n)

def pack4(w):
    words, scales = pack_weight(w, "e2m1")
    return words.reshape(words.shape[0], 128, -1), scales


def unpack4(words, scales):
    return unpack_weight(words.reshape(words.shape[0], 128, -1, 2), scales, "e2m1")


B, IN, H, NS, SS, CS, NA = 6144, 256, 1024, 4, 4, 32, 3
NC = NS * CS


def setup_inputs():
    s = mx_kscale(H)
    h = bf(np.tanh(np.random.standard_normal((B, H))) * s)
    act_logits = bf(np.random.standard_normal((B, NS * NA)) * 1.5)
    stacks = bf(np.random.standard_normal((B, NS, SS, CS)) * 1.5)
    W_push = np.random.standard_normal((NC, H)) * 5.0 / np.sqrt(H) / s
    W_push_words, W_push_scales = pack4(np.ascontiguousarray(W_push.T))
    b_push = bf(np.random.standard_normal(NC) * 0.7)
    return {
        "h": h,
        "act_logits": act_logits,
        "stacks": stacks,
        "W_push_words": W_push_words,
        "W_push_scales": W_push_scales,
        "b_push": b_push,
    }


def reference(h, act_logits, stacks, W_push_words, W_push_scales, b_push):
    st = f64(stacks)
    push = ((mxq(f64(h), 1, "e4m3") @ unpack4(W_push_words, W_push_scales)) + f64(b_push)).reshape(B, NS, CS)
    lg = f64(act_logits)
    e = np.exp(lg - lg.max(-1, keepdims=True))
    act = (e / e.sum(-1, keepdims=True)).reshape(B, NS, NA)
    pa, po, no = act[..., 0][..., None], act[..., 1][..., None], act[..., 2][..., None]
    top_new = pa * push + po * st[:, :, 1, :] + no * st[:, :, 0, :]
    zeros_tail = np.zeros((B, NS, 1, CS))
    pop_rest = np.concatenate([st[:, :, 2:, :], zeros_tail], axis=2)
    rest = (pa[:, :, :, None] * st[:, :, :-1, :]
            + po[:, :, :, None] * pop_rest
            + no[:, :, :, None] * st[:, :, 1:, :])
    return np.concatenate([top_new[:, :, None, :], rest], axis=2)

@@ -1,0 +1,266 @@
+from contextlib import ExitStack
+
+import concourse.mybir as mybir
+from concourse.masks import make_identity
+
+F32 = mybir.dt.float32
+BF16 = mybir.dt.bfloat16
+I32 = mybir.dt.int32
+U32 = mybir.dt.uint32
+U8 = mybir.dt.uint8
+FP8X4 = mybir.dt.float8_e4m3fn_x4
+FP4X4 = mybir.dt.float4_e2m1fn_x4
+ADD = mybir.AluOpType.add
+SUBTRACT = mybir.AluOpType.subtract
+MULT = mybir.AluOpType.mult
+MAX = mybir.AluOpType.max
+COPY = mybir.ActivationFunctionType.Copy
+EXP = mybir.ActivationFunctionType.Exp
+INNERMOST = mybir.AxisListType.X
+
+P = 128
+ROWS = 6144
+TILES = ROWS // P
+HIDDEN = 1024
+K_PASS = 4 * P
+PASSES = HIDDEN // K_PASS
+STACKS = 4
+CELL = 32
+DEPTH = 4
+STACK = DEPTH * CELL
+ROW = STACKS * STACK
+PUSH = STACKS * CELL
+ACTIONS = 3
+LOGITS = STACKS * ACTIONS
+
+FLOPS = 2 * ROWS * HIDDEN * PUSH
+
+CHUNK = 2
+CHUNKS = TILES // CHUNK
+AHEAD = 4
+
+STAGES = 7
+
+
+def tile_stackrnncore_pa_t_kernel(
+    tc, h, act_logits, stacks, W_push_words, W_push_scales, b_push, out
+):
+    nc = tc.nc
+    h_rows = h.rearrange("(p u) k -> p u k", u=TILES)
+    stack_rows = stacks.rearrange("(p u) n i c -> p u (n i c)", u=TILES)
+    out_rows = out.rearrange("(p u) n i c -> p u (n i c)", u=TILES)
+    logit_rows = act_logits.rearrange("(p u) a -> p (u a)", u=TILES)
+
+    with ExitStack() as ctx:
+        const = ctx.enter_context(tc.tile_pool(name="const", bufs=1))
+        h_pool = ctx.enter_context(tc.tile_pool(name="h_pool", bufs=AHEAD + 2))
+        stack_pool = ctx.enter_context(tc.tile_pool(name="stack_pool", bufs=AHEAD + 5))
+        out_pool = ctx.enter_context(tc.tile_pool(name="out_pool", bufs=4))
+        work = ctx.enter_context(tc.tile_pool(name="work", bufs=3))
+        turned_pool = ctx.enter_context(tc.psum_pool(name="turned_pool", bufs=3))
+        push_pool = ctx.enter_context(tc.psum_pool(name="push_pool", bufs=3))
+        ctx.enter_context(tc.manual_schedule())
+
+        h_of = {}
+        stack_of = {}
+        out_of = {}
+        turned_of = {}
+        grouped_of = {}
+        codes_of = {}
+        push_of = {}
+        biased_of = {}
+
+        def load(c):
+            if c >= CHUNKS:
+                return
+            tiles = slice(c * CHUNK, (c + 1) * CHUNK)
+            h_sb = h_pool.tile([P, CHUNK, HIDDEN], BF16, name="h_sb")
+            nc.sync.dma_start(out=h_sb[:], in_=h_rows[:, tiles, :])
+            h_of[c] = h_sb
+            stack_sb = stack_pool.tile([P, CHUNK, ROW], BF16, name="stack_sb")
+            nc.sync.dma_start(out=stack_sb[:], in_=stack_rows[:, tiles, :])
+            stack_of[c] = stack_sb
+
+        logits = const.tile([P, TILES * LOGITS], BF16, name="logits")
+        nc.scalar.dma_start(out=logits[:], in_=logit_rows)
+        bias = const.tile([P, PUSH], BF16, name="bias")
+        nc.scalar.dma_start(out=bias[:], in_=b_push.partition_broadcast(P))
+
+        load(0)
+
+        w_scales = const.tile([P, PASSES * PUSH], U8, name="w_scales", align_bytes=64)
+        nc.vector.memset(w_scales[:].bitcast(I32), 0)
+        for quadrant in range(4):
+            nc.sync.dma_start(
+                out=w_scales[32 * quadrant : 32 * quadrant + 4, :]
+                .rearrange("r (g n) -> r g n", g=PASSES)
+                .bitcast(I32),
+                in_=W_push_scales[:, 4 * quadrant : 4 * quadrant + 4, :]
+                .rearrange("g r n -> r g n")
+                .bitcast(I32),
+            )
+        w_words = const.tile([P, PASSES * 2 * PUSH], U8, name="w_words", align_bytes=64)
+        nc.sync.dma_start(
+            out=w_words[:].rearrange("p (g b) -> p g b", g=PASSES).bitcast(I32),
+            in_=W_push_words.rearrange("g p b -> p g b").bitcast(I32),
+        )
+        for c in range(1, AHEAD):
+            load(c)
+
+        identity = const.tile([P, P], F32, name="identity")
+        make_identity(nc, identity[:])
+
+        by_row = "p (u a) -> p u a"
+        top = const.tile([P, TILES], F32, name="top")
+        nc.vector.tensor_reduce(
+            out=top[:], in_=logits[:].rearrange(by_row, a=LOGITS), axis=INNERMOST, op=MAX
+        )
+        shifted = const.tile([P, TILES * LOGITS], F32, name="shifted")
+        nc.vector.tensor_tensor(
+            out=shifted[:].rearrange(by_row, a=LOGITS),
+            in0=logits[:].rearrange(by_row, a=LOGITS),
+            in1=top[:].unsqueeze(2).to_broadcast([P, TILES, LOGITS]),
+            op=SUBTRACT,
+        )
+        raised = const.tile([P, TILES * LOGITS], F32, name="raised")
+        nc.scalar.activation(out=raised[:], in_=shifted[:], func=EXP)
+        total = const.tile([P, TILES], F32, name="total")
+        nc.vector.tensor_reduce(
+            out=total[:], in_=raised[:].rearrange(by_row, a=LOGITS), axis=INNERMOST, op=ADD
+        )
+        inverse = const.tile([P, TILES], F32, name="inverse")
+        nc.vector.reciprocal(out=inverse[:], in_=total[:])
+        weights = const.tile([P, TILES * LOGITS], F32, name="weights")
+        nc.vector.tensor_tensor(
+            out=weights[:].rearrange(by_row, a=LOGITS),
+            in0=raised[:].rearrange(by_row, a=LOGITS),
+            in1=inverse[:].unsqueeze(2).to_broadcast([P, TILES, LOGITS]),
+            op=MULT,
+        )
+
+        def weight(u, n, action):
+            column = u * LOGITS + n * ACTIONS + action
+            return weights[:, column : column + 1]
+
+        def transpose(u):
+            if not 0 <= u < TILES:
+                return
+            h_words = h_of[u // CHUNK][:, u % CHUNK, :].bitcast(F32)
+            turned = turned_pool.tile([P, PASSES * 2 * P], F32, name="turned")
+            for g in range(PASSES):
+                for w in range(2):
+                    nc.tensor.transpose(
+                        turned[:, (2 * g + w) * P : (2 * g + w + 1) * P],
+                        h_words[:, 2 * P * g + w : 2 * P * (g + 1) : 2],
+                        identity[:],
+                    )
+            turned_of[u] = turned
+
+        def regroup(u):
+            if not 0 <= u < TILES:
+                return
+            grouped = work.tile([P, PASSES * P * 4], BF16, name="grouped", align_bytes=64)
+            nc.scalar.copy(
+                out=grouped[:].bitcast(F32).rearrange("p (g r w) -> p g r w", g=PASSES, w=2),
+                in_=turned_of[u][:].rearrange("p (g w r) -> p g r w", g=PASSES, w=2),
+            )
+            grouped_of[u] = grouped
+
+        def quantise(u):
+            if not 0 <= u < TILES:
+                return
+            codes = work.tile([P, PASSES * P], U32, name="codes", align_bytes=64)
+            h_scales = work.tile([P, PASSES * P], U8, name="h_scales", align_bytes=64)
+            nc.vector.quantize_mx(
+                out=codes[:].bitcast(FP8X4), scales=h_scales[:], in_=grouped_of[u][:]
+            )
+            codes_of[u] = (codes, h_scales)
+
+        def project(u):
+            if not 0 <= u < TILES:
+                return
+            codes, h_scales = codes_of[u]
+            push = push_pool.tile([P, PUSH], F32, name="push")
+            for g in range(PASSES):
+                nc.tensor.matmul_mx(
+                    out=push[:],
+                    lhsT=codes[:, g * P : (g + 1) * P].bitcast(FP8X4),
+                    lhsT_scale=h_scales[:, g * P : (g + 1) * P],
+                    rhs=w_words[:, g * 2 * PUSH : (g + 1) * 2 * PUSH].bitcast(FP4X4),
+                    rhs_scale=w_scales[:, g * PUSH : (g + 1) * PUSH],
+                    start=(g == 0),
+                    stop=(g == PASSES - 1),
+                )
+            push_of[u] = push
+
+        def add_bias(u):
+            if not 0 <= u < TILES:
+                return
+            biased = work.tile([P, PUSH], F32, name="biased")
+            nc.vector.tensor_tensor(out=biased[:], in0=push_of[u][:], in1=bias[:], op=ADD)
+            biased_of[u] = biased
+
+        def start_blend(u):
+            if not 0 <= u < TILES:
+                return
+            c, j = u // CHUNK, u % CHUNK
+            if j == 0:
+                out_sb = out_pool.tile([P, CHUNK, ROW], F32, name="out_sb")
+                out_of[c] = out_sb
+            for n in range(STACKS):
+                first = n * STACK
+                nc.scalar.activation(
+                    out=out_of[c][:, j, first + CELL : first + STACK],
+                    in_=stack_of[c][:, j, first : first + STACK - CELL],
+                    func=COPY,
+                    scale=weight(u, n, 0),
+                )
+            for n in range(STACKS):
+                first = n * STACK
+                nc.scalar.activation(
+                    out=out_of[c][:, j, first : first + CELL],
+                    in_=biased_of[u][:, n * CELL : (n + 1) * CELL],
+                    func=COPY,
+                    scale=weight(u, n, 0),
+                )
+
+        def finish_blend(u):
+            if not 0 <= u < TILES:
+                return
+            c, j = u // CHUNK, u % CHUNK
+            for n in range(STACKS):
+                cells = slice(n * STACK, (n + 1) * STACK)
+                nc.vector.scalar_tensor_tensor(
+                    out=out_of[c][:, j, cells],
+                    in0=stack_of[c][:, j, cells],
+                    scalar=weight(u, n, 2),
+                    in1=out_of[c][:, j, cells],
+                    op0=MULT,
+                    op1=ADD,
+                )
+            for n in range(STACKS):
+                first = n * STACK
+                upper = slice(first, first + STACK - CELL)
+                nc.vector.scalar_tensor_tensor(
+                    out=out_of[c][:, j, upper],
+                    in0=stack_of[c][:, j, first + CELL : first + STACK],
+                    scalar=weight(u, n, 1),
+                    in1=out_of[c][:, j, upper],
+                    op0=MULT,
+                    op1=ADD,
+                )
+            if j == CHUNK - 1:
+                nc.sync.dma_start(
+                    out=out_rows[:, c * CHUNK : (c + 1) * CHUNK, :], in_=out_of[c][:]
+                )
+
+        for step in range(TILES + STAGES - 1):
+            if step % CHUNK == 0:
+                load(step // CHUNK + AHEAD)
+            transpose(step)
+            regroup(step - 1)
+            quantise(step - 2)
+            project(step - 3)
+            add_bias(step - 4)
+            start_blend(step - 5)
+            finish_blend(step - 6)

@@ -35,9 +35,9 @@ LOGITS = STACKS * ACTIONS
 
 FLOPS = 2 * ROWS * HIDDEN * PUSH
 
-CHUNK = 2
+CHUNK = 4
 CHUNKS = TILES // CHUNK
-AHEAD = 4
+AHEAD = 2
 
 STAGES = 7
 
@@ -54,8 +54,8 @@ def tile_stackrnncore_pa_t_kernel(
     with ExitStack() as ctx:
         const = ctx.enter_context(tc.tile_pool(name="const", bufs=1))
         h_pool = ctx.enter_context(tc.tile_pool(name="h_pool", bufs=AHEAD + 2))
-        stack_pool = ctx.enter_context(tc.tile_pool(name="stack_pool", bufs=AHEAD + 5))
-        out_pool = ctx.enter_context(tc.tile_pool(name="out_pool", bufs=4))
+        stack_pool = ctx.enter_context(tc.tile_pool(name="stack_pool", bufs=AHEAD + 4))
+        out_pool = ctx.enter_context(tc.tile_pool(name="out_pool", bufs=3))
         work = ctx.enter_context(tc.tile_pool(name="work", bufs=3))
         turned_pool = ctx.enter_context(tc.psum_pool(name="turned_pool", bufs=3))
         push_pool = ctx.enter_context(tc.psum_pool(name="push_pool", bufs=3))

@@ -15,6 +15,7 @@ SUBTRACT = mybir.AluOpType.subtract
 MULT = mybir.AluOpType.mult
 MAX = mybir.AluOpType.max
 COPY = mybir.ActivationFunctionType.Copy
+IDENTITY = mybir.ActivationFunctionType.Identity
 EXP = mybir.ActivationFunctionType.Exp
 INNERMOST = mybir.AxisListType.X
 
@@ -35,11 +36,12 @@ LOGITS = STACKS * ACTIONS
 
 FLOPS = 2 * ROWS * HIDDEN * PUSH
 
-CHUNK = 4
+CHUNK = 2
 CHUNKS = TILES // CHUNK
-AHEAD = 2
+AHEAD = 4
 
-STAGES = 7
+STEPS_PER_TILE = 6
+FIRST_STEPS = 3
 
 
 def tile_stackrnncore_pa_t_kernel(
@@ -54,11 +56,12 @@ def tile_stackrnncore_pa_t_kernel(
     with ExitStack() as ctx:
         const = ctx.enter_context(tc.tile_pool(name="const", bufs=1))
         h_pool = ctx.enter_context(tc.tile_pool(name="h_pool", bufs=AHEAD + 2))
-        stack_pool = ctx.enter_context(tc.tile_pool(name="stack_pool", bufs=AHEAD + 4))
-        out_pool = ctx.enter_context(tc.tile_pool(name="out_pool", bufs=3))
+        stack_pool = ctx.enter_context(tc.tile_pool(name="stack_pool", bufs=AHEAD + 2 + (STEPS_PER_TILE + CHUNK - 2) // CHUNK))
+        out_pool = ctx.enter_context(tc.tile_pool(name="out_pool", bufs=4))
         work = ctx.enter_context(tc.tile_pool(name="work", bufs=3))
         turned_pool = ctx.enter_context(tc.psum_pool(name="turned_pool", bufs=3))
-        push_pool = ctx.enter_context(tc.psum_pool(name="push_pool", bufs=3))
+        push_pool = ctx.enter_context(tc.psum_pool(name="push_pool", bufs=2))
+        biased_pool = ctx.enter_context(tc.psum_pool(name="biased_pool", bufs=3))
         ctx.enter_context(tc.manual_schedule())
 
         h_of = {}
@@ -68,6 +71,7 @@ def tile_stackrnncore_pa_t_kernel(
         grouped_of = {}
         codes_of = {}
         push_of = {}
+        sideways_of = {}
         biased_of = {}
 
         def load(c):
@@ -82,9 +86,9 @@ def tile_stackrnncore_pa_t_kernel(
             stack_of[c] = stack_sb
 
         logits = const.tile([P, TILES * LOGITS], BF16, name="logits")
-        nc.scalar.dma_start(out=logits[:], in_=logit_rows)
-        bias = const.tile([P, PUSH], BF16, name="bias")
-        nc.scalar.dma_start(out=bias[:], in_=b_push.partition_broadcast(P))
+        nc.sync.dma_start(out=logits[:], in_=logit_rows)
+        bias = const.tile([P, 1], BF16, name="bias")
+        nc.scalar.dma_start(out=bias[:], in_=b_push.rearrange("(p o) -> p o", o=1))
 
         load(0)
 
@@ -124,19 +128,21 @@ def tile_stackrnncore_pa_t_kernel(
         )
         raised = const.tile([P, TILES * LOGITS], F32, name="raised")
         nc.scalar.activation(out=raised[:], in_=shifted[:], func=EXP)
-        total = const.tile([P, TILES], F32, name="total")
-        nc.vector.tensor_reduce(
-            out=total[:], in_=raised[:].rearrange(by_row, a=LOGITS), axis=INNERMOST, op=ADD
-        )
-        inverse = const.tile([P, TILES], F32, name="inverse")
-        nc.vector.reciprocal(out=inverse[:], in_=total[:])
         weights = const.tile([P, TILES * LOGITS], F32, name="weights")
-        nc.vector.tensor_tensor(
-            out=weights[:].rearrange(by_row, a=LOGITS),
-            in0=raised[:].rearrange(by_row, a=LOGITS),
-            in1=inverse[:].unsqueeze(2).to_broadcast([P, TILES, LOGITS]),
-            op=MULT,
-        )
+
+        def normalise():
+            total = const.tile([P, TILES], F32, name="total")
+            nc.vector.tensor_reduce(
+                out=total[:], in_=raised[:].rearrange(by_row, a=LOGITS), axis=INNERMOST, op=ADD
+            )
+            inverse = const.tile([P, TILES], F32, name="inverse")
+            nc.vector.reciprocal(out=inverse[:], in_=total[:])
+            nc.vector.tensor_tensor(
+                out=weights[:].rearrange(by_row, a=LOGITS),
+                in0=raised[:].rearrange(by_row, a=LOGITS),
+                in1=inverse[:].unsqueeze(2).to_broadcast([P, TILES, LOGITS]),
+                op=MULT,
+            )
 
         def weight(u, n, action):
             column = u * LOGITS + n * ACTIONS + action
@@ -180,14 +186,14 @@ def tile_stackrnncore_pa_t_kernel(
             if not 0 <= u < TILES:
                 return
             codes, h_scales = codes_of[u]
-            push = push_pool.tile([P, PUSH], F32, name="push")
+            push = push_pool.tile([PUSH, P], F32, name="push")
             for g in range(PASSES):
                 nc.tensor.matmul_mx(
                     out=push[:],
-                    lhsT=codes[:, g * P : (g + 1) * P].bitcast(FP8X4),
-                    lhsT_scale=h_scales[:, g * P : (g + 1) * P],
-                    rhs=w_words[:, g * 2 * PUSH : (g + 1) * 2 * PUSH].bitcast(FP4X4),
-                    rhs_scale=w_scales[:, g * PUSH : (g + 1) * PUSH],
+                    lhsT=w_words[:, g * 2 * PUSH : (g + 1) * 2 * PUSH].bitcast(FP4X4),
+                    lhsT_scale=w_scales[:, g * PUSH : (g + 1) * PUSH],
+                    rhs=codes[:, g * P : (g + 1) * P].bitcast(FP8X4),
+                    rhs_scale=h_scales[:, g * P : (g + 1) * P],
                     start=(g == 0),
                     stop=(g == PASSES - 1),
                 )
@@ -196,8 +202,15 @@ def tile_stackrnncore_pa_t_kernel(
         def add_bias(u):
             if not 0 <= u < TILES:
                 return
-            biased = work.tile([P, PUSH], F32, name="biased")
-            nc.vector.tensor_tensor(out=biased[:], in0=push_of[u][:], in1=bias[:], op=ADD)
+            sideways = work.tile([PUSH, P], F32, name="sideways")
+            nc.scalar.activation(out=sideways[:], in_=push_of[u][:], func=IDENTITY, bias=bias[:])
+            sideways_of[u] = sideways
+
+        def turn_back(u):
+            if not 0 <= u < TILES:
+                return
+            biased = biased_pool.tile([P, PUSH], F32, name="biased")
+            nc.tensor.transpose(biased[:], sideways_of[u][:], identity[:])
             biased_of[u] = biased
 
         def start_blend(u):
@@ -254,13 +267,20 @@ def tile_stackrnncore_pa_t_kernel(
                     out=out_rows[:, c * CHUNK : (c + 1) * CHUNK, :], in_=out_of[c][:]
                 )
 
-        for step in range(TILES + STAGES - 1):
+        def take_step(step):
             if step % CHUNK == 0:
                 load(step // CHUNK + AHEAD)
             transpose(step)
             regroup(step - 1)
             quantise(step - 2)
-            project(step - 3)
-            add_bias(step - 4)
-            start_blend(step - 5)
-            finish_blend(step - 6)
+            project(step - 2)
+            add_bias(step - 3)
+            turn_back(step - 3)
+            start_blend(step - 4)
+            finish_blend(step - 5)
+
+        for step in range(FIRST_STEPS):
+            take_step(step)
+        normalise()
+        for step in range(FIRST_STEPS, TILES + STEPS_PER_TILE - 1):
+            take_step(step)

@@ -58,6 +58,7 @@ def tile_stackrnncore_pa_t_kernel(
         h_pool = ctx.enter_context(tc.tile_pool(name="h_pool", bufs=AHEAD + 2))
         stack_pool = ctx.enter_context(tc.tile_pool(name="stack_pool", bufs=AHEAD + 2 + (STEPS_PER_TILE + CHUNK - 2) // CHUNK))
         out_pool = ctx.enter_context(tc.tile_pool(name="out_pool", bufs=4))
+        first_pool = ctx.enter_context(tc.tile_pool(name="first_pool", bufs=4))
         work = ctx.enter_context(tc.tile_pool(name="work", bufs=3))
         turned_pool = ctx.enter_context(tc.psum_pool(name="turned_pool", bufs=3))
         push_pool = ctx.enter_context(tc.psum_pool(name="push_pool", bufs=2))
@@ -67,6 +68,7 @@ def tile_stackrnncore_pa_t_kernel(
         h_of = {}
         stack_of = {}
         out_of = {}
+        first_of = {}
         turned_of = {}
         grouped_of = {}
         codes_of = {}
@@ -220,10 +222,12 @@ def tile_stackrnncore_pa_t_kernel(
             if j == 0:
                 out_sb = out_pool.tile([P, CHUNK, ROW], F32, name="out_sb")
                 out_of[c] = out_sb
+            first_sb = first_pool.tile([P, ROW], F32, name="first_sb")
+            first_of[u] = first_sb
             for n in range(STACKS):
                 first = n * STACK
                 nc.scalar.activation(
-                    out=out_of[c][:, j, first + CELL : first + STACK],
+                    out=first_sb[:, first + CELL : first + STACK],
                     in_=stack_of[c][:, j, first : first + STACK - CELL],
                     func=COPY,
                     scale=weight(u, n, 0),
@@ -231,7 +235,7 @@ def tile_stackrnncore_pa_t_kernel(
             for n in range(STACKS):
                 first = n * STACK
                 nc.scalar.activation(
-                    out=out_of[c][:, j, first : first + CELL],
+                    out=first_sb[:, first : first + CELL],
                     in_=biased_of[u][:, n * CELL : (n + 1) * CELL],
                     func=COPY,
                     scale=weight(u, n, 0),
@@ -247,7 +251,7 @@ def tile_stackrnncore_pa_t_kernel(
                     out=out_of[c][:, j, cells],
                     in0=stack_of[c][:, j, cells],
                     scalar=weight(u, n, 2),
-                    in1=out_of[c][:, j, cells],
+                    in1=first_of[u][:, cells],
                     op0=MULT,
                     op1=ADD,
                 )

@@ -266,7 +266,17 @@ def tile_stackrnncore_pa_t_kernel(
                     op0=MULT,
                     op1=ADD,
                 )
-            if j == CHUNK - 1:
+                if u == TILES - 1 and n >= 1:
+                    piece = slice((n - 1 if n == 1 else n) * STACK, (n + 1) * STACK)
+                    nc.sync.dma_start(
+                        out=out_rows[:, u : u + 1, piece], in_=out_of[c][:, j : j + 1, piece]
+                    )
+            if c == CHUNKS - 1:
+                if u < TILES - 1:
+                    nc.sync.dma_start(
+                        out=out_rows[:, u : u + 1, :], in_=out_of[c][:, j : j + 1, :]
+                    )
+            elif j == CHUNK - 1:
                 nc.sync.dma_start(
                     out=out_rows[:, c * CHUNK : (c + 1) * CHUNK, :], in_=out_of[c][:]
                 )

@@ -41,7 +41,7 @@ CHUNKS = TILES // CHUNK
 AHEAD = 4
 
 STEPS_PER_TILE = 6
-FIRST_STEPS = 3
+SOON = 8
 
 
 def tile_stackrnncore_pa_t_kernel(
@@ -92,7 +92,21 @@ def tile_stackrnncore_pa_t_kernel(
         bias = const.tile([P, 1], BF16, name="bias")
         nc.scalar.dma_start(out=bias[:], in_=b_push.rearrange("(p o) -> p o", o=1))
 
-        load(0)
+        def load_h_tile(u):
+            c, j = u // CHUNK, u % CHUNK
+            if j == 0:
+                h_sb = h_pool.tile([P, CHUNK, HIDDEN], BF16, name="h_sb")
+                h_of[c] = h_sb
+            nc.sync.dma_start(out=h_of[c][:, j : j + 1, :], in_=h_rows[:, u : u + 1, :])
+
+        def load_stack_tile(u):
+            c, j = u // CHUNK, u % CHUNK
+            if j == 0:
+                stack_sb = stack_pool.tile([P, CHUNK, ROW], BF16, name="stack_sb")
+                stack_of[c] = stack_sb
+            nc.sync.dma_start(out=stack_of[c][:, j : j + 1, :], in_=stack_rows[:, u : u + 1, :])
+
+        load_h_tile(0)
 
         w_scales = const.tile([P, PASSES * PUSH], U8, name="w_scales", align_bytes=64)
         nc.vector.memset(w_scales[:].bitcast(I32), 0)
@@ -110,41 +124,75 @@ def tile_stackrnncore_pa_t_kernel(
             out=w_words[:].rearrange("p (g b) -> p g b", g=PASSES).bitcast(I32),
             in_=W_push_words.rearrange("g p b -> p g b").bitcast(I32),
         )
-        for c in range(1, AHEAD):
+        load_h_tile(1)
+        load_h_tile(2)
+        load_stack_tile(0)
+        load_h_tile(3)
+        load_stack_tile(1)
+        load_stack_tile(2)
+        load_stack_tile(3)
+        for c in range(2, AHEAD):
             load(c)
 
         identity = const.tile([P, P], F32, name="identity")
         make_identity(nc, identity[:])
 
-        by_row = "p (u a) -> p u a"
         top = const.tile([P, TILES], F32, name="top")
-        nc.vector.tensor_reduce(
-            out=top[:], in_=logits[:].rearrange(by_row, a=LOGITS), axis=INNERMOST, op=MAX
-        )
         shifted = const.tile([P, TILES * LOGITS], F32, name="shifted")
-        nc.vector.tensor_tensor(
-            out=shifted[:].rearrange(by_row, a=LOGITS),
-            in0=logits[:].rearrange(by_row, a=LOGITS),
-            in1=top[:].unsqueeze(2).to_broadcast([P, TILES, LOGITS]),
-            op=SUBTRACT,
-        )
         raised = const.tile([P, TILES * LOGITS], F32, name="raised")
-        nc.scalar.activation(out=raised[:], in_=shifted[:], func=EXP)
+        total = const.tile([P, TILES], F32, name="total")
+        inverse = const.tile([P, TILES], F32, name="inverse")
         weights = const.tile([P, TILES * LOGITS], F32, name="weights")
 
-        def normalise():
-            total = const.tile([P, TILES], F32, name="total")
-            nc.vector.tensor_reduce(
-                out=total[:], in_=raised[:].rearrange(by_row, a=LOGITS), axis=INNERMOST, op=ADD
+        def by_row(flat, tiles):
+            return flat[:, tiles.start * LOGITS : tiles.stop * LOGITS].rearrange(
+                "p (u a) -> p u a", a=LOGITS
             )
-            inverse = const.tile([P, TILES], F32, name="inverse")
-            nc.vector.reciprocal(out=inverse[:], in_=total[:])
+
+        def spread(one_per_row, tiles):
+            return (
+                one_per_row[:, tiles]
+                .unsqueeze(2)
+                .to_broadcast([P, tiles.stop - tiles.start, LOGITS])
+            )
+
+        def find_top(tiles):
+            nc.vector.tensor_reduce(
+                out=top[:, tiles], in_=by_row(logits, tiles), axis=INNERMOST, op=MAX
+            )
+
+        def shift(tiles):
             nc.vector.tensor_tensor(
-                out=weights[:].rearrange(by_row, a=LOGITS),
-                in0=raised[:].rearrange(by_row, a=LOGITS),
-                in1=inverse[:].unsqueeze(2).to_broadcast([P, TILES, LOGITS]),
+                out=by_row(shifted, tiles),
+                in0=by_row(logits, tiles),
+                in1=spread(top, tiles),
+                op=SUBTRACT,
+            )
+
+        def raise_e(tiles):
+            columns = slice(tiles.start * LOGITS, tiles.stop * LOGITS)
+            nc.scalar.activation(out=raised[:, columns], in_=shifted[:, columns], func=EXP)
+
+        def normalise(tiles):
+            nc.vector.tensor_reduce(
+                out=total[:, tiles], in_=by_row(raised, tiles), axis=INNERMOST, op=ADD
+            )
+            nc.vector.reciprocal(out=inverse[:, tiles], in_=total[:, tiles])
+            nc.vector.tensor_tensor(
+                out=by_row(weights, tiles),
+                in0=by_row(raised, tiles),
+                in1=spread(inverse, tiles),
                 op=MULT,
             )
+
+        soon = slice(0, SOON)
+        later = slice(SOON, TILES)
+        find_top(soon)
+        shift(soon)
+        raise_e(soon)
+        normalise(soon)
+        find_top(later)
+        shift(later)
 
         def weight(u, n, action):
             column = u * LOGITS + n * ACTIONS + action
@@ -215,7 +263,7 @@ def tile_stackrnncore_pa_t_kernel(
             nc.tensor.transpose(biased[:], sideways_of[u][:], identity[:])
             biased_of[u] = biased
 
-        def start_blend(u):
+        def scale_cells(u):
             if not 0 <= u < TILES:
                 return
             c, j = u // CHUNK, u % CHUNK
@@ -232,10 +280,15 @@ def tile_stackrnncore_pa_t_kernel(
                     func=COPY,
                     scale=weight(u, n, 0),
                 )
+
+        def scale_top(u):
+            if not 0 <= u < TILES:
+                return
+            c, j = u // CHUNK, u % CHUNK
             for n in range(STACKS):
                 first = n * STACK
                 nc.scalar.activation(
-                    out=first_sb[:, first : first + CELL],
+                    out=first_of[u][:, first : first + CELL],
                     in_=biased_of[u][:, n * CELL : (n + 1) * CELL],
                     func=COPY,
                     scale=weight(u, n, 0),
@@ -290,11 +343,13 @@ def tile_stackrnncore_pa_t_kernel(
             project(step - 2)
             add_bias(step - 3)
             turn_back(step - 3)
-            start_blend(step - 4)
+            scale_cells(step - 4)
+            scale_top(step - 4)
             finish_blend(step - 5)
 
-        for step in range(FIRST_STEPS):
+        for step in range(TILES + STEPS_PER_TILE - 1):
             take_step(step)
-        normalise()
-        for step in range(FIRST_STEPS, TILES + STEPS_PER_TILE - 1):
-            take_step(step)
+            if step == 2:
+                raise_e(later)
+            if step == 3:
+                normalise(later)

@@ -107,6 +107,7 @@ def tile_stackrnncore_pa_t_kernel(
             nc.sync.dma_start(out=stack_of[c][:, j : j + 1, :], in_=stack_rows[:, u : u + 1, :])
 
         load_h_tile(0)
+        load_h_tile(1)
 
         w_scales = const.tile([P, PASSES * PUSH], U8, name="w_scales", align_bytes=64)
         nc.vector.memset(w_scales[:].bitcast(I32), 0)
@@ -124,7 +125,6 @@ def tile_stackrnncore_pa_t_kernel(
             out=w_words[:].rearrange("p (g b) -> p g b", g=PASSES).bitcast(I32),
             in_=W_push_words.rearrange("g p b -> p g b").bitcast(I32),
         )
-        load_h_tile(1)
         load_h_tile(2)
         load_stack_tile(0)
         load_h_tile(3)
@@ -187,12 +187,11 @@ def tile_stackrnncore_pa_t_kernel(
 
         soon = slice(0, SOON)
         later = slice(SOON, TILES)
-        find_top(soon)
+        find_top(slice(0, TILES))
         shift(soon)
         raise_e(soon)
-        normalise(soon)
-        find_top(later)
         shift(later)
+        normalise(soon)
 
         def weight(u, n, action):
             column = u * LOGITS + n * ACTIONS + action

@@ -56,8 +56,8 @@ def tile_stackrnncore_pa_t_kernel(
     with ExitStack() as ctx:
         const = ctx.enter_context(tc.tile_pool(name="const", bufs=1))
         h_pool = ctx.enter_context(tc.tile_pool(name="h_pool", bufs=AHEAD + 2))
-        stack_pool = ctx.enter_context(tc.tile_pool(name="stack_pool", bufs=AHEAD + 2 + (STEPS_PER_TILE + CHUNK - 2) // CHUNK))
-        out_pool = ctx.enter_context(tc.tile_pool(name="out_pool", bufs=4))
+        stack_pool = ctx.enter_context(tc.tile_pool(name="stack_pool", bufs=CHUNKS))
+        out_pool = ctx.enter_context(tc.tile_pool(name="out_pool", bufs=CHUNKS))
         first_pool = ctx.enter_context(tc.tile_pool(name="first_pool", bufs=4))
         work = ctx.enter_context(tc.tile_pool(name="work", bufs=3))
         turned_pool = ctx.enter_context(tc.psum_pool(name="turned_pool", bufs=3))

@@ -37,11 +37,13 @@ LOGITS = STACKS * ACTIONS
 FLOPS = 2 * ROWS * HIDDEN * PUSH
 
 CHUNK = 2
+STACK_CHUNK = 4
 CHUNKS = TILES // CHUNK
 AHEAD = 4
 
 STEPS_PER_TILE = 6
 SOON = 8
+HELPED = 1
 
 
 def tile_stackrnncore_pa_t_kernel(
@@ -56,9 +58,10 @@ def tile_stackrnncore_pa_t_kernel(
     with ExitStack() as ctx:
         const = ctx.enter_context(tc.tile_pool(name="const", bufs=1))
         h_pool = ctx.enter_context(tc.tile_pool(name="h_pool", bufs=AHEAD + 2))
-        stack_pool = ctx.enter_context(tc.tile_pool(name="stack_pool", bufs=CHUNKS))
+        stack_pool = ctx.enter_context(tc.tile_pool(name="stack_pool", bufs=TILES // STACK_CHUNK))
         out_pool = ctx.enter_context(tc.tile_pool(name="out_pool", bufs=CHUNKS))
         first_pool = ctx.enter_context(tc.tile_pool(name="first_pool", bufs=4))
+        below_pool = ctx.enter_context(tc.tile_pool(name="below_pool", bufs=HELPED))
         work = ctx.enter_context(tc.tile_pool(name="work", bufs=3))
         turned_pool = ctx.enter_context(tc.psum_pool(name="turned_pool", bufs=3))
         push_pool = ctx.enter_context(tc.psum_pool(name="push_pool", bufs=2))
@@ -69,6 +72,7 @@ def tile_stackrnncore_pa_t_kernel(
         stack_of = {}
         out_of = {}
         first_of = {}
+        below_of = {}
         turned_of = {}
         grouped_of = {}
         codes_of = {}
@@ -83,9 +87,12 @@ def tile_stackrnncore_pa_t_kernel(
             h_sb = h_pool.tile([P, CHUNK, HIDDEN], BF16, name="h_sb")
             nc.sync.dma_start(out=h_sb[:], in_=h_rows[:, tiles, :])
             h_of[c] = h_sb
-            stack_sb = stack_pool.tile([P, CHUNK, ROW], BF16, name="stack_sb")
-            nc.sync.dma_start(out=stack_sb[:], in_=stack_rows[:, tiles, :])
-            stack_of[c] = stack_sb
+            if tiles.stop % STACK_CHUNK == 0:
+                tiles = slice(tiles.stop - STACK_CHUNK, tiles.stop)
+                stack_sb = stack_pool.tile([P, STACK_CHUNK, ROW], BF16, name="stack_sb")
+                nc.sync.dma_start(out=stack_sb[:], in_=stack_rows[:, tiles, :])
+                for u in range(tiles.start, tiles.stop):
+                    stack_of[u] = stack_sb[:, u - tiles.start, :]
 
         logits = const.tile([P, TILES * LOGITS], BF16, name="logits")
         nc.sync.dma_start(out=logits[:], in_=logit_rows)
@@ -99,12 +106,11 @@ def tile_stackrnncore_pa_t_kernel(
                 h_of[c] = h_sb
             nc.sync.dma_start(out=h_of[c][:, j : j + 1, :], in_=h_rows[:, u : u + 1, :])
 
+        first_stacks = stack_pool.tile([P, STACK_CHUNK, ROW], BF16, name="stack_sb")
+
         def load_stack_tile(u):
-            c, j = u // CHUNK, u % CHUNK
-            if j == 0:
-                stack_sb = stack_pool.tile([P, CHUNK, ROW], BF16, name="stack_sb")
-                stack_of[c] = stack_sb
-            nc.sync.dma_start(out=stack_of[c][:, j : j + 1, :], in_=stack_rows[:, u : u + 1, :])
+            nc.sync.dma_start(out=first_stacks[:, u : u + 1, :], in_=stack_rows[:, u : u + 1, :])
+            stack_of[u] = first_stacks[:, u, :]
 
         load_h_tile(0)
         load_h_tile(1)
@@ -275,10 +281,31 @@ def tile_stackrnncore_pa_t_kernel(
                 first = n * STACK
                 nc.scalar.activation(
                     out=first_sb[:, first + CELL : first + STACK],
-                    in_=stack_of[c][:, j, first : first + STACK - CELL],
+                    in_=stack_of[u][:, first : first + STACK - CELL],
                     func=COPY,
                     scale=weight(u, n, 0),
                 )
+
+        def scale_below(u):
+            if not TILES - HELPED <= u < TILES:
+                return
+            below = below_pool.tile([P, STACKS, STACK - CELL], F32, name="below")
+            below_of[u] = below
+            for n in range(STACKS):
+                first = n * STACK
+                nc.scalar.activation(
+                    out=below[:, n, :],
+                    in_=stack_of[u][:, first + CELL : first + STACK],
+                    func=COPY,
+                    scale=weight(u, n, 1),
+                )
+
+        def join_terms(u):
+            if u not in below_of:
+                return
+            for half in (slice(0, STACKS // 2), slice(STACKS // 2, STACKS)):
+                upper = first_of[u][:].rearrange("p (n s) -> p n s", n=STACKS)[:, half, : STACK - CELL]
+                nc.vector.tensor_tensor(out=upper, in0=upper, in1=below_of[u][:, half, :], op=ADD)
 
         def scale_top(u):
             if not 0 <= u < TILES:
@@ -301,20 +328,9 @@ def tile_stackrnncore_pa_t_kernel(
                 cells = slice(n * STACK, (n + 1) * STACK)
                 nc.vector.scalar_tensor_tensor(
                     out=out_of[c][:, j, cells],
-                    in0=stack_of[c][:, j, cells],
+                    in0=stack_of[u][:, cells],
                     scalar=weight(u, n, 2),
                     in1=first_of[u][:, cells],
-                    op0=MULT,
-                    op1=ADD,
-                )
-            for n in range(STACKS):
-                first = n * STACK
-                upper = slice(first, first + STACK - CELL)
-                nc.vector.scalar_tensor_tensor(
-                    out=out_of[c][:, j, upper],
-                    in0=stack_of[c][:, j, first + CELL : first + STACK],
-                    scalar=weight(u, n, 1),
-                    in1=out_of[c][:, j, upper],
                     op0=MULT,
                     op1=ADD,
                 )
@@ -323,6 +339,19 @@ def tile_stackrnncore_pa_t_kernel(
                     nc.sync.dma_start(
                         out=out_rows[:, u : u + 1, piece], in_=out_of[c][:, j : j + 1, piece]
                     )
+            for n in range(STACKS):
+                if u in below_of:
+                    break
+                first = n * STACK
+                upper = slice(first, first + STACK - CELL)
+                nc.vector.scalar_tensor_tensor(
+                    out=out_of[c][:, j, upper],
+                    in0=stack_of[u][:, first + CELL : first + STACK],
+                    scalar=weight(u, n, 1),
+                    in1=out_of[c][:, j, upper],
+                    op0=MULT,
+                    op1=ADD,
+                )
             if c == CHUNKS - 1:
                 if u < TILES - 1:
                     nc.sync.dma_start(
@@ -337,13 +366,15 @@ def tile_stackrnncore_pa_t_kernel(
             if step % CHUNK == 0:
                 load(step // CHUNK + AHEAD)
             transpose(step)
+            scale_cells(step - 4)
+            scale_below(step - 4)
             regroup(step - 1)
             quantise(step - 2)
             project(step - 2)
             add_bias(step - 3)
             turn_back(step - 3)
-            scale_cells(step - 4)
             scale_top(step - 4)
+            join_terms(step - 5)
             finish_blend(step - 5)
 
         for step in range(TILES + STEPS_PER_TILE - 1):

@@ -80,40 +80,38 @@ def tile_stackrnncore_pa_t_kernel(
         sideways_of = {}
         biased_of = {}
 
+        def load_h(c):
+            h_sb = h_pool.tile([P, CHUNK, HIDDEN], BF16, name="h_sb")
+            nc.sync.dma_start(out=h_sb[:], in_=h_rows[:, c * CHUNK : (c + 1) * CHUNK, :])
+            h_of[c] = h_sb
+
+        def load_stacks(s):
+            tiles = slice(s * STACK_CHUNK, (s + 1) * STACK_CHUNK)
+            stack_sb = stack_pool.tile([P, STACK_CHUNK, ROW], BF16, name="stack_sb")
+            nc.sync.dma_start(out=stack_sb[:], in_=stack_rows[:, tiles, :])
+            for u in range(tiles.start, tiles.stop):
+                stack_of[u] = stack_sb[:, u - tiles.start, :]
+
         def load(c):
             if c >= CHUNKS:
                 return
-            tiles = slice(c * CHUNK, (c + 1) * CHUNK)
-            h_sb = h_pool.tile([P, CHUNK, HIDDEN], BF16, name="h_sb")
-            nc.sync.dma_start(out=h_sb[:], in_=h_rows[:, tiles, :])
-            h_of[c] = h_sb
-            if tiles.stop % STACK_CHUNK == 0:
-                tiles = slice(tiles.stop - STACK_CHUNK, tiles.stop)
-                stack_sb = stack_pool.tile([P, STACK_CHUNK, ROW], BF16, name="stack_sb")
-                nc.sync.dma_start(out=stack_sb[:], in_=stack_rows[:, tiles, :])
-                for u in range(tiles.start, tiles.stop):
-                    stack_of[u] = stack_sb[:, u - tiles.start, :]
+            load_h(c)
+            if (c + 1) * CHUNK % STACK_CHUNK == 0:
+                load_stacks((c + 1) * CHUNK // STACK_CHUNK - 1)
 
         logits = const.tile([P, TILES * LOGITS], BF16, name="logits")
         nc.sync.dma_start(out=logits[:], in_=logit_rows)
-        bias = const.tile([P, 1], BF16, name="bias")
-        nc.scalar.dma_start(out=bias[:], in_=b_push.rearrange("(p o) -> p o", o=1))
 
-        def load_h_tile(u):
-            c, j = u // CHUNK, u % CHUNK
-            if j == 0:
-                h_sb = h_pool.tile([P, CHUNK, HIDDEN], BF16, name="h_sb")
-                h_of[c] = h_sb
-            nc.sync.dma_start(out=h_of[c][:, j : j + 1, :], in_=h_rows[:, u : u + 1, :])
-
-        first_stacks = stack_pool.tile([P, STACK_CHUNK, ROW], BF16, name="stack_sb")
-
-        def load_stack_tile(u):
-            nc.sync.dma_start(out=first_stacks[:, u : u + 1, :], in_=stack_rows[:, u : u + 1, :])
-            stack_of[u] = first_stacks[:, u, :]
-
-        load_h_tile(0)
-        load_h_tile(1)
+        h_first = h_pool.tile([P, CHUNK, HIDDEN], BF16, name="h_sb")
+        h_of[0] = h_first
+        nc.sync.dma_start(out=h_first[:, 0:1, :], in_=h_rows[:, 0:1, :])
+        w_words = const.tile([P, PASSES * 2 * PUSH], U8, name="w_words", align_bytes=64)
+        nc.sync.dma_start(
+            out=w_words[:].rearrange("p (g b) -> p g b", g=PASSES).bitcast(I32),
+            in_=W_push_words.rearrange("g p b -> p g b").bitcast(I32),
+        )
+        nc.sync.dma_start(out=h_first[:, 1:2, :], in_=h_rows[:, 1:2, :])
+        load_h(1)
 
         w_scales = const.tile([P, PASSES * PUSH], U8, name="w_scales", align_bytes=64)
         nc.vector.memset(w_scales[:].bitcast(I32), 0)
@@ -126,17 +124,9 @@ def tile_stackrnncore_pa_t_kernel(
                 .rearrange("g r n -> r g n")
                 .bitcast(I32),
             )
-        w_words = const.tile([P, PASSES * 2 * PUSH], U8, name="w_words", align_bytes=64)
-        nc.sync.dma_start(
-            out=w_words[:].rearrange("p (g b) -> p g b", g=PASSES).bitcast(I32),
-            in_=W_push_words.rearrange("g p b -> p g b").bitcast(I32),
-        )
-        load_h_tile(2)
-        load_stack_tile(0)
-        load_h_tile(3)
-        load_stack_tile(1)
-        load_stack_tile(2)
-        load_stack_tile(3)
+        bias = const.tile([P, 1], BF16, name="bias")
+        nc.sync.dma_start(out=bias[:], in_=b_push.rearrange("(p o) -> p o", o=1))
+        load_stacks(0)
         for c in range(2, AHEAD):
             load(c)
 

@@ -39,7 +39,7 @@ FLOPS = 2 * ROWS * HIDDEN * PUSH
 CHUNK = 2
 STACK_CHUNK = 4
 CHUNKS = TILES // CHUNK
-AHEAD = 4
+AHEAD = 2
 
 STEPS_PER_TILE = 6
 SOON = 8
@@ -57,7 +57,7 @@ def tile_stackrnncore_pa_t_kernel(
 
     with ExitStack() as ctx:
         const = ctx.enter_context(tc.tile_pool(name="const", bufs=1))
-        h_pool = ctx.enter_context(tc.tile_pool(name="h_pool", bufs=AHEAD + 2))
+        h_pool = ctx.enter_context(tc.tile_pool(name="h_pool", bufs=6))
         stack_pool = ctx.enter_context(tc.tile_pool(name="stack_pool", bufs=TILES // STACK_CHUNK))
         out_pool = ctx.enter_context(tc.tile_pool(name="out_pool", bufs=CHUNKS))
         first_pool = ctx.enter_context(tc.tile_pool(name="first_pool", bufs=4))

from contextlib import ExitStack

import concourse.mybir as mybir
from concourse.masks import make_identity

F32 = mybir.dt.float32
BF16 = mybir.dt.bfloat16
I32 = mybir.dt.int32
U32 = mybir.dt.uint32
U8 = mybir.dt.uint8
FP8X4 = mybir.dt.float8_e4m3fn_x4
FP4X4 = mybir.dt.float4_e2m1fn_x4
ADD = mybir.AluOpType.add
SUBTRACT = mybir.AluOpType.subtract
MULT = mybir.AluOpType.mult
MAX = mybir.AluOpType.max
COPY = mybir.ActivationFunctionType.Copy
IDENTITY = mybir.ActivationFunctionType.Identity
EXP = mybir.ActivationFunctionType.Exp
INNERMOST = mybir.AxisListType.X

P = 128
ROWS = 6144
TILES = ROWS // P
HIDDEN = 1024
K_PASS = 4 * P
PASSES = HIDDEN // K_PASS
STACKS = 4
CELL = 32
DEPTH = 4
STACK = DEPTH * CELL
ROW = STACKS * STACK
PUSH = STACKS * CELL
ACTIONS = 3
LOGITS = STACKS * ACTIONS

FLOPS = 2 * ROWS * HIDDEN * PUSH

CHUNK = 2
STACK_CHUNK = 4
CHUNKS = TILES // CHUNK
AHEAD = 2

STEPS_PER_TILE = 6
SOON = 8
HELPED = 1


def tile_stackrnncore_pa_t_kernel(
    tc, h, act_logits, stacks, W_push_words, W_push_scales, b_push, out
):
    nc = tc.nc
    h_rows = h.rearrange("(p u) k -> p u k", u=TILES)
    stack_rows = stacks.rearrange("(p u) n i c -> p u (n i c)", u=TILES)
    out_rows = out.rearrange("(p u) n i c -> p u (n i c)", u=TILES)
    logit_rows = act_logits.rearrange("(p u) a -> p (u a)", u=TILES)

    with ExitStack() as ctx:
        const = ctx.enter_context(tc.tile_pool(name="const", bufs=1))
        h_pool = ctx.enter_context(tc.tile_pool(name="h_pool", bufs=6))
        stack_pool = ctx.enter_context(tc.tile_pool(name="stack_pool", bufs=TILES // STACK_CHUNK))
        out_pool = ctx.enter_context(tc.tile_pool(name="out_pool", bufs=CHUNKS))
        first_pool = ctx.enter_context(tc.tile_pool(name="first_pool", bufs=4))
        below_pool = ctx.enter_context(tc.tile_pool(name="below_pool", bufs=HELPED))
        work = ctx.enter_context(tc.tile_pool(name="work", bufs=3))
        turned_pool = ctx.enter_context(tc.psum_pool(name="turned_pool", bufs=3))
        push_pool = ctx.enter_context(tc.psum_pool(name="push_pool", bufs=2))
        biased_pool = ctx.enter_context(tc.psum_pool(name="biased_pool", bufs=3))
        ctx.enter_context(tc.manual_schedule())

        h_of = {}
        stack_of = {}
        out_of = {}
        first_of = {}
        below_of = {}
        turned_of = {}
        grouped_of = {}
        codes_of = {}
        push_of = {}
        sideways_of = {}
        biased_of = {}

        def load_h(c):
            h_sb = h_pool.tile([P, CHUNK, HIDDEN], BF16, name="h_sb")
            nc.sync.dma_start(out=h_sb[:], in_=h_rows[:, c * CHUNK : (c + 1) * CHUNK, :])
            h_of[c] = h_sb

        def load_stacks(s):
            tiles = slice(s * STACK_CHUNK, (s + 1) * STACK_CHUNK)
            stack_sb = stack_pool.tile([P, STACK_CHUNK, ROW], BF16, name="stack_sb")
            nc.sync.dma_start(out=stack_sb[:], in_=stack_rows[:, tiles, :])
            for u in range(tiles.start, tiles.stop):
                stack_of[u] = stack_sb[:, u - tiles.start, :]

        def load(c):
            if c >= CHUNKS:
                return
            load_h(c)
            if (c + 1) * CHUNK % STACK_CHUNK == 0:
                load_stacks((c + 1) * CHUNK // STACK_CHUNK - 1)

        logits = const.tile([P, TILES * LOGITS], BF16, name="logits")
        nc.sync.dma_start(out=logits[:], in_=logit_rows)

        h_first = h_pool.tile([P, CHUNK, HIDDEN], BF16, name="h_sb")
        h_of[0] = h_first
        nc.sync.dma_start(out=h_first[:, 0:1, :], in_=h_rows[:, 0:1, :])
        w_words = const.tile([P, PASSES * 2 * PUSH], U8, name="w_words", align_bytes=64)
        nc.sync.dma_start(
            out=w_words[:].rearrange("p (g b) -> p g b", g=PASSES).bitcast(I32),
            in_=W_push_words.rearrange("g p b -> p g b").bitcast(I32),
        )
        nc.sync.dma_start(out=h_first[:, 1:2, :], in_=h_rows[:, 1:2, :])
        load_h(1)

        w_scales = const.tile([P, PASSES * PUSH], U8, name="w_scales", align_bytes=64)
        nc.vector.memset(w_scales[:].bitcast(I32), 0)
        for quadrant in range(4):
            nc.sync.dma_start(
                out=w_scales[32 * quadrant : 32 * quadrant + 4, :]
                .rearrange("r (g n) -> r g n", g=PASSES)
                .bitcast(I32),
                in_=W_push_scales[:, 4 * quadrant : 4 * quadrant + 4, :]
                .rearrange("g r n -> r g n")
                .bitcast(I32),
            )
        bias = const.tile([P, 1], BF16, name="bias")
        nc.sync.dma_start(out=bias[:], in_=b_push.rearrange("(p o) -> p o", o=1))
        load_stacks(0)
        for c in range(2, AHEAD):
            load(c)

        identity = const.tile([P, P], F32, name="identity")
        make_identity(nc, identity[:])

        top = const.tile([P, TILES], F32, name="top")
        shifted = const.tile([P, TILES * LOGITS], F32, name="shifted")
        raised = const.tile([P, TILES * LOGITS], F32, name="raised")
        total = const.tile([P, TILES], F32, name="total")
        inverse = const.tile([P, TILES], F32, name="inverse")
        weights = const.tile([P, TILES * LOGITS], F32, name="weights")

        def by_row(flat, tiles):
            return flat[:, tiles.start * LOGITS : tiles.stop * LOGITS].rearrange(
                "p (u a) -> p u a", a=LOGITS
            )

        def spread(one_per_row, tiles):
            return (
                one_per_row[:, tiles]
                .unsqueeze(2)
                .to_broadcast([P, tiles.stop - tiles.start, LOGITS])
            )

        def find_top(tiles):
            nc.vector.tensor_reduce(
                out=top[:, tiles], in_=by_row(logits, tiles), axis=INNERMOST, op=MAX
            )

        def shift(tiles):
            nc.vector.tensor_tensor(
                out=by_row(shifted, tiles),
                in0=by_row(logits, tiles),
                in1=spread(top, tiles),
                op=SUBTRACT,
            )

        def raise_e(tiles):
            columns = slice(tiles.start * LOGITS, tiles.stop * LOGITS)
            nc.scalar.activation(out=raised[:, columns], in_=shifted[:, columns], func=EXP)

        def normalise(tiles):
            nc.vector.tensor_reduce(
                out=total[:, tiles], in_=by_row(raised, tiles), axis=INNERMOST, op=ADD
            )
            nc.vector.reciprocal(out=inverse[:, tiles], in_=total[:, tiles])
            nc.vector.tensor_tensor(
                out=by_row(weights, tiles),
                in0=by_row(raised, tiles),
                in1=spread(inverse, tiles),
                op=MULT,
            )

        soon = slice(0, SOON)
        later = slice(SOON, TILES)
        find_top(slice(0, TILES))
        shift(soon)
        raise_e(soon)
        shift(later)
        normalise(soon)

        def weight(u, n, action):
            column = u * LOGITS + n * ACTIONS + action
            return weights[:, column : column + 1]

        def transpose(u):
            if not 0 <= u < TILES:
                return
            h_words = h_of[u // CHUNK][:, u % CHUNK, :].bitcast(F32)
            turned = turned_pool.tile([P, PASSES * 2 * P], F32, name="turned")
            for g in range(PASSES):
                for w in range(2):
                    nc.tensor.transpose(
                        turned[:, (2 * g + w) * P : (2 * g + w + 1) * P],
                        h_words[:, 2 * P * g + w : 2 * P * (g + 1) : 2],
                        identity[:],
                    )
            turned_of[u] = turned

        def regroup(u):
            if not 0 <= u < TILES:
                return
            grouped = work.tile([P, PASSES * P * 4], BF16, name="grouped", align_bytes=64)
            nc.scalar.copy(
                out=grouped[:].bitcast(F32).rearrange("p (g r w) -> p g r w", g=PASSES, w=2),
                in_=turned_of[u][:].rearrange("p (g w r) -> p g r w", g=PASSES, w=2),
            )
            grouped_of[u] = grouped

        def quantise(u):
            if not 0 <= u < TILES:
                return
            codes = work.tile([P, PASSES * P], U32, name="codes", align_bytes=64)
            h_scales = work.tile([P, PASSES * P], U8, name="h_scales", align_bytes=64)
            nc.vector.quantize_mx(
                out=codes[:].bitcast(FP8X4), scales=h_scales[:], in_=grouped_of[u][:]
            )
            codes_of[u] = (codes, h_scales)

        def project(u):
            if not 0 <= u < TILES:
                return
            codes, h_scales = codes_of[u]
            push = push_pool.tile([PUSH, P], F32, name="push")
            for g in range(PASSES):
                nc.tensor.matmul_mx(
                    out=push[:],
                    lhsT=w_words[:, g * 2 * PUSH : (g + 1) * 2 * PUSH].bitcast(FP4X4),
                    lhsT_scale=w_scales[:, g * PUSH : (g + 1) * PUSH],
                    rhs=codes[:, g * P : (g + 1) * P].bitcast(FP8X4),
                    rhs_scale=h_scales[:, g * P : (g + 1) * P],
                    start=(g == 0),
                    stop=(g == PASSES - 1),
                )
            push_of[u] = push

        def add_bias(u):
            if not 0 <= u < TILES:
                return
            sideways = work.tile([PUSH, P], F32, name="sideways")
            nc.scalar.activation(out=sideways[:], in_=push_of[u][:], func=IDENTITY, bias=bias[:])
            sideways_of[u] = sideways

        def turn_back(u):
            if not 0 <= u < TILES:
                return
            biased = biased_pool.tile([P, PUSH], F32, name="biased")
            nc.tensor.transpose(biased[:], sideways_of[u][:], identity[:])
            biased_of[u] = biased

        def scale_cells(u):
            if not 0 <= u < TILES:
                return
            c, j = u // CHUNK, u % CHUNK
            if j == 0:
                out_sb = out_pool.tile([P, CHUNK, ROW], F32, name="out_sb")
                out_of[c] = out_sb
            first_sb = first_pool.tile([P, ROW], F32, name="first_sb")
            first_of[u] = first_sb
            for n in range(STACKS):
                first = n * STACK
                nc.scalar.activation(
                    out=first_sb[:, first + CELL : first + STACK],
                    in_=stack_of[u][:, first : first + STACK - CELL],
                    func=COPY,
                    scale=weight(u, n, 0),
                )

        def scale_below(u):
            if not TILES - HELPED <= u < TILES:
                return
            below = below_pool.tile([P, STACKS, STACK - CELL], F32, name="below")
            below_of[u] = below
            for n in range(STACKS):
                first = n * STACK
                nc.scalar.activation(
                    out=below[:, n, :],
                    in_=stack_of[u][:, first + CELL : first + STACK],
                    func=COPY,
                    scale=weight(u, n, 1),
                )

        def join_terms(u):
            if u not in below_of:
                return
            for half in (slice(0, STACKS // 2), slice(STACKS // 2, STACKS)):
                upper = first_of[u][:].rearrange("p (n s) -> p n s", n=STACKS)[:, half, : STACK - CELL]
                nc.vector.tensor_tensor(out=upper, in0=upper, in1=below_of[u][:, half, :], op=ADD)

        def scale_top(u):
            if not 0 <= u < TILES:
                return
            c, j = u // CHUNK, u % CHUNK
            for n in range(STACKS):
                first = n * STACK
                nc.scalar.activation(
                    out=first_of[u][:, first : first + CELL],
                    in_=biased_of[u][:, n * CELL : (n + 1) * CELL],
                    func=COPY,
                    scale=weight(u, n, 0),
                )

        def finish_blend(u):
            if not 0 <= u < TILES:
                return
            c, j = u // CHUNK, u % CHUNK
            for n in range(STACKS):
                cells = slice(n * STACK, (n + 1) * STACK)
                nc.vector.scalar_tensor_tensor(
                    out=out_of[c][:, j, cells],
                    in0=stack_of[u][:, cells],
                    scalar=weight(u, n, 2),
                    in1=first_of[u][:, cells],
                    op0=MULT,
                    op1=ADD,
                )
                if u == TILES - 1 and n >= 1:
                    piece = slice((n - 1 if n == 1 else n) * STACK, (n + 1) * STACK)
                    nc.sync.dma_start(
                        out=out_rows[:, u : u + 1, piece], in_=out_of[c][:, j : j + 1, piece]
                    )
            for n in range(STACKS):
                if u in below_of:
                    break
                first = n * STACK
                upper = slice(first, first + STACK - CELL)
                nc.vector.scalar_tensor_tensor(
                    out=out_of[c][:, j, upper],
                    in0=stack_of[u][:, first + CELL : first + STACK],
                    scalar=weight(u, n, 1),
                    in1=out_of[c][:, j, upper],
                    op0=MULT,
                    op1=ADD,
                )
            if c == CHUNKS - 1:
                if u < TILES - 1:
                    nc.sync.dma_start(
                        out=out_rows[:, u : u + 1, :], in_=out_of[c][:, j : j + 1, :]
                    )
            elif j == CHUNK - 1:
                nc.sync.dma_start(
                    out=out_rows[:, c * CHUNK : (c + 1) * CHUNK, :], in_=out_of[c][:]
                )

        def take_step(step):
            if step % CHUNK == 0:
                load(step // CHUNK + AHEAD)
            transpose(step)
            scale_cells(step - 4)
            scale_below(step - 4)
            regroup(step - 1)
            quantise(step - 2)
            project(step - 2)
            add_bias(step - 3)
            turn_back(step - 3)
            scale_top(step - 4)
            join_terms(step - 5)
            finish_blend(step - 5)

        for step in range(TILES + STEPS_PER_TILE - 1):
            take_step(step)
            if step == 2:
                raise_e(later)
            if step == 3:
                normalise(later)
